import numpy as np
import ml_dtypes


def mxq(x, axis, fmt="e4m3"):
    dtype, down = {"e4m3": (ml_dtypes.float8_e4m3fn, 7), "e5m2": (ml_dtypes.float8_e5m2, 14)}[fmt]
    v = np.moveaxis(np.asarray(x, np.float32).astype(ml_dtypes.bfloat16).astype(np.float64), axis, -1)
    blocks = v.reshape(v.shape[:-1] + (-1, 32))
    amax = np.abs(blocks).max(-1, keepdims=True)
    byte = np.maximum(np.where(amax > 0, np.frexp(amax)[1] - 1 + 127, 0) - down, 1)
    scale = np.exp2(byte - 127.0)
    codes = (blocks / scale).astype(np.float32).astype(dtype).astype(np.float64)
    return np.moveaxis((codes * scale).reshape(v.shape), -1, axis)


WIDE = False


def mx_kscale(k):
    if not WIDE:
        return np.ones(k)
    levels = np.array([10, -10, 5, -5, 0])
    if k % 512:
        return np.exp2(np.random.permutation(np.resize(levels, k // 32))).repeat(32)
    a = np.empty((k // 512, 16))
    for p in range(k // 512):
        a[p, :8] = np.random.permutation(np.resize(levels, 8))
        for g in range(8):
            far = levels[np.abs(levels - a[p, g]) >= 10]
            a[p, g + 8] = far[np.random.randint(len(far))]
    return np.exp2(a.ravel()).repeat(32)


BF16 = ml_dtypes.bfloat16


def bf(x):
    return np.asarray(x, np.float32).astype(BF16)


def f64(x):
    return np.asarray(x).astype(np.float64)


N, D, DO, R0, R1, R2, R3, R4 = 2560, 512, 512, 1, 2, 4, 10, 25
SCALES = (R0, R1, R2, R3)
NS = len(SCALES)


def setup_inputs():
    s = mx_kscale(D)
    return {"inputs_c_e": bf(np.random.standard_normal((N, D)) * s),
            "Ws": bf(np.random.standard_normal((NS, DO, D)) / np.sqrt(D) / s),
            "bs": bf(np.random.standard_normal((NS, DO)) * 0.5)}


def reference(inputs_c_e, Ws, bs):
    x, W, b = f64(inputs_c_e), f64(Ws), f64(bs)
    outs = []
    for i, r in enumerate(SCALES):
        groups = N // r
        sums = x.reshape(groups, r, D).sum(axis=1)
        h = np.maximum((mxq(sums, 1, "e4m3") @ mxq(W[i].T, 0, "e4m3")) + b[i], 0.0) / r
        outs.append(np.repeat(h, r, axis=0))
    return np.concatenate(outs, axis=0)

@@ -1,0 +1,294 @@
+from contextlib import ExitStack
+
+import concourse.mybir as mybir
+from concourse.masks import make_identity
+
+F32 = mybir.dt.float32
+BF16 = mybir.dt.bfloat16
+U32 = mybir.dt.uint32
+U8 = mybir.dt.uint8
+FP8X4 = mybir.dt.float8_e4m3fn_x4
+ADD = mybir.AluOpType.add
+MULT = mybir.AluOpType.mult
+RELU = mybir.ActivationFunctionType.Relu
+
+P = 128
+ROWS = 2560
+K = 512
+OUT = 512
+GROUP = (1, 2, 4, 10)
+TILES = ROWS // P
+CHUNK = 4
+CHUNKS = TILES // CHUNK
+PSUM_BANK = 512
+PRODUCT_BANKS = 5
+FLOPS = 2 * sum(ROWS // r for r in GROUP) * K * OUT
+
+
+def tile_contractexpand_pa_kernel(tc, inputs_c_e, Ws, bs, out):
+    nc = tc.nc
+    x_rows = inputs_c_e.rearrange("(p t) k -> p (t k)", t=TILES)
+    w_rows = Ws.rearrange("i (p c) k -> i p (c k)", c=4)
+    bias_row = bs.rearrange("(o i) d -> o (i d)", o=1)
+    out_rows = out.rearrange("(i p t) d -> i p t d", i=len(GROUP), t=TILES)
+
+    with ExitStack() as ctx:
+        keep = ctx.enter_context(tc.tile_pool(name="keep", bufs=1))
+        w_pool = ctx.enter_context(tc.tile_pool(name="w_pool", bufs=2))
+        out_pool = ctx.enter_context(tc.tile_pool(name="out_pool", bufs=6))
+        flip_pool = ctx.enter_context(tc.psum_pool(name="flip_pool", bufs=8 - PRODUCT_BANKS))
+        product_pool = ctx.enter_context(tc.psum_pool(name="product_pool", bufs=PRODUCT_BANKS))
+        ctx.enter_context(tc.manual_schedule())
+
+        identity = keep.tile([P, P], F32, name="identity")
+        ones = keep.tile([P, P], BF16, name="ones")
+        bias_in = keep.tile([P, len(GROUP) * OUT], BF16, name="bias_in")
+        bias = keep.tile([P, len(GROUP), OUT], F32, name="bias")
+        x_in = [keep.tile([P, CHUNK * K], BF16, name="x_in%d" % j) for j in range(CHUNKS)]
+        w_in = {}
+        x_t = [keep.tile([P, CHUNK * K], BF16, name="x_t%d" % j, align_bytes=64) for j in range(CHUNKS)]
+        w_t = [keep.tile([P, 4 * OUT], BF16, name="w_t%d" % i, align_bytes=64) for i in range(len(GROUP))]
+        pair_f32 = [keep.tile([P, 2, K], F32, name="pair_f32_%d" % j) for j in range(CHUNKS)]
+        pair_t = [keep.tile([P, 2 * K], BF16, name="pair_t%d" % j, align_bytes=64) for j in range(CHUNKS)]
+        quad_f32 = dict((j, keep.tile([P, K], F32, name="quad_f32_%d" % j)) for j in (0, 1, 3, 4))
+        quad_t = [keep.tile([P, K], BF16, name="quad_t%d" % j, align_bytes=64) for j in range(CHUNKS)]
+        eight_f32 = [keep.tile([P, K], F32, name="eight_f32_%d" % g) for g in range(2)]
+        ten_t = [keep.tile([P, K], BF16, name="ten_t%d" % g, align_bytes=64) for g in range(2)]
+        w_codes = [keep.tile([P, OUT], U32, name="w_codes%d" % i, align_bytes=64) for i in range(len(GROUP))]
+        w_scales = [keep.tile([P, OUT], U8, name="w_scales%d" % i, align_bytes=64) for i in range(len(GROUP))]
+        widths = (CHUNK * P, 2 * P, P, P)
+        counts = (CHUNKS, CHUNKS, CHUNKS, 2)
+        codes = [
+            [keep.tile([P, widths[i]], U32, name="codes%d_%d" % (i, n), align_bytes=64) for n in range(counts[i])]
+            for i in range(len(GROUP))
+        ]
+        scales = [
+            [keep.tile([P, widths[i]], U8, name="scales%d_%d" % (i, n), align_bytes=64) for n in range(counts[i])]
+            for i in range(len(GROUP))
+        ]
+        quad_row = [keep.tile([P, 1, OUT], F32, name="quad_row%d" % j) for j in range(CHUNKS)]
+        ten_row = [keep.tile([P, 1, OUT], F32, name="ten_row%d" % g) for g in range(2)]
+        ten_rows = keep.tile([P, 5, OUT], F32, name="ten_rows")
+        products = {}
+        out_tiles = {}
+
+        def load_x(j, first, last):
+            nc.sync.dma_start(
+                out=x_in[j][:, first * K : last * K], in_=x_rows[:, (j * CHUNK + first) * K : (j * CHUNK + last) * K]
+            )
+
+        def load_w(i):
+            w_tile = w_pool.tile([P, 4 * K], BF16, name="w_tile", tag="w_tile")
+            w_in[i] = w_tile
+            nc.sync.dma_start(out=w_tile[:], in_=w_rows[i])
+
+        def flip(source, half):
+            words = source[:].bitcast(F32)
+            bank = flip_pool.tile([P, PSUM_BANK], F32, name="bank", tag="bank")
+            for m in range(4):
+                first = (2 * half + m // 2) * (K // 2)
+                nc.tensor.transpose(
+                    bank[:, m * P : (m + 1) * P], words[:, first + m % 2 : first + K // 2 : 2], identity[:]
+                )
+            return bank
+
+        def flip_x(j, half):
+            bank = flip(x_in[j], half)
+            nc.scalar.copy(
+                out=x_t[j][:].bitcast(F32).rearrange("q (t p u) -> q t p u", t=CHUNK, u=2)[
+                    :, 2 * half : 2 * half + 2, :, :
+                ],
+                in_=bank[:].rearrange("q (t u p) -> q t p u", t=2, u=2),
+            )
+
+        def unpack_w(i, half, bank):
+            nc.scalar.copy(
+                out=w_t[i][:].bitcast(F32).rearrange("q (p h m) -> q p h m", h=2, m=4)[:, :, half, :],
+                in_=bank[:].rearrange("q (m p) -> q p m", m=4),
+            )
+
+        def flip_w(i, half):
+            unpack_w(i, half, flip(w_in[i], half))
+
+        def spread_bias(i):
+            spread = product_pool.tile([P, OUT], F32, name="spread", tag="product")
+            nc.tensor.matmul(out=spread[:], lhsT=ones[:], rhs=bias_in[:, i * OUT : (i + 1) * OUT], start=True, stop=True)
+            nc.scalar.copy(out=bias[:, i, :], in_=spread[:])
+
+        def add(dst, a, b):
+            nc.vector.tensor_tensor(out=dst, in0=a, in1=b, op=ADD)
+
+        def pool_copy(dst, src):
+            nc.gpsimd.tensor_scalar(out=dst, in0=src, scalar1=1.0, scalar2=0.0, op0=MULT, op1=ADD)
+
+        def sum_pairs(j):
+            tiles = x_t[j][:].rearrange("q (g two n) -> q g two n", g=2, two=2)
+            add(pair_f32[j][:], tiles[:, :, 0, :], tiles[:, :, 1, :])
+
+        def sum_quad(j, dst):
+            add(dst[:], pair_f32[j][:, 0, :], pair_f32[j][:, 1, :])
+
+        def quantise(i, n, source):
+            nc.vector.quantize_mx(out=codes[i][n][:].bitcast(FP8X4), scales=scales[i][n][:], in_=source[:])
+
+        def quantise_w(i):
+            nc.vector.quantize_mx(out=w_codes[i][:].bitcast(FP8X4), scales=w_scales[i][:], in_=w_t[i][:])
+
+        def multiply(i, n):
+            per_tile = widths[i] // P
+            cols = slice((n % per_tile) * P, (n % per_tile + 1) * P)
+            product = product_pool.tile([P, OUT], F32, name="product", tag="product")
+            products[(i, n)] = product
+            nc.tensor.matmul_mx(
+                out=product[:],
+                lhsT=codes[i][n // per_tile][:, cols].bitcast(FP8X4),
+                lhsT_scale=scales[i][n // per_tile][:, cols],
+                rhs=w_codes[i][:].bitcast(FP8X4),
+                rhs_scale=w_scales[i][:],
+                start=True,
+                stop=True,
+            )
+
+        def add_bias(i, n, dst):
+            add(dst, products[(i, n)][:], bias[:, i, :])
+
+        def relu(i, dst, src):
+            nc.scalar.activation(out=dst, in_=src, func=RELU, scale=1.0 / GROUP[i])
+
+        def store(i, first, src):
+            nc.sync.dma_start(out=out_rows[i, :, first : first + src.shape[1], :], in_=src)
+
+        def finish_row(i, first, row, cuts):
+            relu(i, row[:], row[:])
+            for count in cuts:
+                store(i, first, row[:].to_broadcast([P, count, OUT]))
+                first += count
+
+        def finish_quad(j):
+            rows = out_pool.tile([P, CHUNK, OUT], F32, name="rows", tag="rows")
+            relu(2, rows[:], quad_row[j][:].to_broadcast([P, CHUNK, OUT]))
+            store(2, j * CHUNK, rows[:])
+
+        nc.vector.memset(bias_in[:], 0.0)
+        nc.vector.memset(ones[:], 1.0)
+        make_identity(nc, identity[:])
+        load_x(0, 0, 2)
+        load_x(0, 2, 4)
+        load_w(2)
+        load_x(1, 0, CHUNK)
+        load_x(2, 0, CHUNK)
+        nc.sync.dma_start(out=bias_in[0:1, :], in_=bias_row)
+        load_w(3)
+        load_x(3, 0, CHUNK)
+        load_x(4, 0, CHUNK)
+
+        flip_x(0, 0)
+        flip_x(0, 1)
+        flip_w(2, 0)
+        flip_w(2, 1)
+        load_w(1)
+        sum_pairs(0)
+        sum_quad(0, quad_t[0])
+        quantise(2, 0, quad_t[0])
+        sum_quad(0, quad_f32[0])
+        quantise_w(2)
+        flip_x(1, 0)
+        flip_x(1, 1)
+        spread_bias(2)
+        flip_x(2, 0)
+        flip_x(2, 1)
+        multiply(2, 0)
+        sum_pairs(1)
+        sum_quad(1, quad_f32[1])
+        pool_copy(quad_t[1][:], quad_f32[1][:])
+        add_bias(2, 0, quad_row[0][:, 0, :])
+        flip_w(3, 0)
+        spread_bias(3)
+        last_bank = flip(w_in[3], 1)
+        load_w(0)
+        finish_row(2, 0, quad_row[0], (CHUNK,))
+        unpack_w(3, 1, last_bank)
+        add(eight_f32[0][:], quad_f32[0][:], quad_f32[1][:])
+        quantise(2, 1, quad_t[1])
+        flip_x(3, 0)
+        multiply(2, 1)
+        flip_x(3, 1)
+        sum_pairs(2)
+        add_bias(2, 1, quad_row[1][:, 0, :])
+        finish_row(2, CHUNK, quad_row[1], (CHUNK,))
+        quantise_w(3)
+        add(ten_t[0][:], eight_f32[0][:], pair_f32[2][:, 0, :])
+        quantise(3, 0, ten_t[0])
+        sum_quad(2, quad_t[2])
+        quantise(2, 2, quad_t[2])
+        flip_x(4, 0)
+        flip_x(4, 1)
+        multiply(3, 0)
+        add_bias(3, 0, ten_row[0][:, 0, :])
+        finish_row(3, 0, ten_row[0], (4, 4, 2))
+        flip_w(1, 0)
+        multiply(2, 2)
+        flip_w(1, 1)
+        flip_w(0, 0)
+        sum_pairs(3)
+        sum_quad(3, quad_f32[3])
+        pool_copy(quad_t[3][:], quad_f32[3][:])
+        add_bias(2, 2, quad_row[2][:, 0, :])
+        finish_quad(2)
+        sum_pairs(4)
+        quantise(2, 3, quad_t[3])
+        multiply(2, 3)
+        sum_quad(4, quad_f32[4])
+        pool_copy(quad_t[4][:], quad_f32[4][:])
+        add(eight_f32[1][:], pair_f32[2][:, 1, :], quad_f32[3][:])
+        add_bias(2, 3, quad_row[3][:, 0, :])
+        finish_quad(3)
+        add(ten_t[1][:], eight_f32[1][:], quad_f32[4][:])
+        quantise(3, 1, ten_t[1])
+        multiply(3, 1)
+        add_bias(3, 1, ten_row[1][:, 0, :])
+        relu(3, ten_rows[:], ten_row[1][:].to_broadcast([P, 5, OUT]))
+        store(3, 10, ten_rows[:])
+        store(3, 15, ten_rows[:])
+        flip_w(0, 1)
+        quantise(2, 4, quad_t[4])
+        multiply(2, 4)
+        spread_bias(1)
+        spread_bias(0)
+        for j in range(CHUNKS):
+            pool_copy(pair_t[j][:], pair_f32[j][:].rearrange("q g n -> q (g n)"))
+        quantise_w(1)
+        quantise(0, 0, x_t[0])
+        quantise(1, 0, pair_t[0])
+        add_bias(2, 4, quad_row[4][:, 0, :])
+        quantise_w(0)
+        finish_quad(4)
+
+        passes = []
+        for j in range(CHUNKS):
+            passes.extend((1, 2 * j + g) for g in range(2))
+            passes.extend((0, CHUNK * j + t) for t in range(CHUNK))
+        for i, n in passes[:PRODUCT_BANKS]:
+            multiply(i, n)
+        for step, (i, n) in enumerate(passes):
+            per_chunk = CHUNK // GROUP[i]
+            j = n // per_chunk
+            place = n % per_chunk
+            if place == 0:
+                rows = out_pool.tile([P, CHUNK, OUT], F32, name="rows", tag="rows")
+                out_tiles[i] = rows
+            rows = out_tiles[i]
+            add_bias(i, n, rows[:, place * GROUP[i], :])
+            if place == 1 and j + 1 < CHUNKS:
+                quantise(i, j + 1, (x_t, pair_t)[i][j + 1])
+            if step + PRODUCT_BANKS < len(passes):
+                multiply(*passes[step + PRODUCT_BANKS])
+            if i == 1 and place == 1:
+                twice = rows[:].rearrange("p (g two) d -> p g two d", two=2)
+                relu(1, twice[:, :, 0, :], twice[:, :, 0, :])
+                pool_copy(twice[:, :, 1, :], twice[:, :, 0, :])
+                store(1, j * CHUNK, rows[:])
+            if i == 0 and place % 2 == 1:
+                relu(0, rows[:, place - 1 : place + 1, :], rows[:, place - 1 : place + 1, :])
+            if i == 0 and place == CHUNK - 1:
+                store(0, j * CHUNK, rows[:])

@@ -9,6 +9,7 @@ U32 = mybir.dt.uint32
 U8 = mybir.dt.uint8
 FP8X4 = mybir.dt.float8_e4m3fn_x4
 ADD = mybir.AluOpType.add
+MAX = mybir.AluOpType.max
 MULT = mybir.AluOpType.mult
 RELU = mybir.ActivationFunctionType.Relu
 
@@ -34,7 +35,11 @@ def tile_contractexpand_pa_kernel(tc, inputs_c_e, Ws, bs, out):
 
     with ExitStack() as ctx:
         keep = ctx.enter_context(tc.tile_pool(name="keep", bufs=1))
-        w_pool = ctx.enter_context(tc.tile_pool(name="w_pool", bufs=2))
+        w_pool = ctx.enter_context(tc.tile_pool(name="w_pool", bufs=3))
+        wt_pool = ctx.enter_context(tc.tile_pool(name="wt_pool", bufs=2))
+        sum_pool = ctx.enter_context(tc.tile_pool(name="sum_pool", bufs=3))
+        row_pool = ctx.enter_context(tc.tile_pool(name="row_pool", bufs=3))
+        ten_pool = ctx.enter_context(tc.tile_pool(name="ten_pool", bufs=2))
         out_pool = ctx.enter_context(tc.tile_pool(name="out_pool", bufs=6))
         flip_pool = ctx.enter_context(tc.psum_pool(name="flip_pool", bufs=8 - PRODUCT_BANKS))
         product_pool = ctx.enter_context(tc.psum_pool(name="product_pool", bufs=PRODUCT_BANKS))
@@ -47,12 +52,13 @@ def tile_contractexpand_pa_kernel(tc, inputs_c_e, Ws, bs, out):
         x_in = [keep.tile([P, CHUNK * K], BF16, name="x_in%d" % j) for j in range(CHUNKS)]
         w_in = {}
         x_t = [keep.tile([P, CHUNK * K], BF16, name="x_t%d" % j, align_bytes=64) for j in range(CHUNKS)]
-        w_t = [keep.tile([P, 4 * OUT], BF16, name="w_t%d" % i, align_bytes=64) for i in range(len(GROUP))]
-        pair_f32 = [keep.tile([P, 2, K], F32, name="pair_f32_%d" % j) for j in range(CHUNKS)]
-        pair_t = [keep.tile([P, 2 * K], BF16, name="pair_t%d" % j, align_bytes=64) for j in range(CHUNKS)]
-        quad_f32 = dict((j, keep.tile([P, K], F32, name="quad_f32_%d" % j)) for j in (0, 1, 3, 4))
+        w_t = {}
+        pair_t = {}
+        pair_f32 = {}
+        quad_f32 = [keep.tile([P, K], F32, name="quad_f32_%d" % j) for j in range(CHUNKS)]
         quad_t = [keep.tile([P, K], BF16, name="quad_t%d" % j, align_bytes=64) for j in range(CHUNKS)]
         eight_f32 = [keep.tile([P, K], F32, name="eight_f32_%d" % g) for g in range(2)]
+        ten_f32 = [keep.tile([P, K], F32, name="ten_f32_%d" % g) for g in range(2)]
         ten_t = [keep.tile([P, K], BF16, name="ten_t%d" % g, align_bytes=64) for g in range(2)]
         w_codes = [keep.tile([P, OUT], U32, name="w_codes%d" % i, align_bytes=64) for i in range(len(GROUP))]
         w_scales = [keep.tile([P, OUT], U8, name="w_scales%d" % i, align_bytes=64) for i in range(len(GROUP))]
@@ -66,21 +72,21 @@ def tile_contractexpand_pa_kernel(tc, inputs_c_e, Ws, bs, out):
             [keep.tile([P, widths[i]], U8, name="scales%d_%d" % (i, n), align_bytes=64) for n in range(counts[i])]
             for i in range(len(GROUP))
         ]
-        quad_row = [keep.tile([P, 1, OUT], F32, name="quad_row%d" % j) for j in range(CHUNKS)]
-        ten_row = [keep.tile([P, 1, OUT], F32, name="ten_row%d" % g) for g in range(2)]
-        ten_rows = keep.tile([P, 5, OUT], F32, name="ten_rows")
         products = {}
         out_tiles = {}
+        single_rows = {}
 
         def load_x(j, first, last):
             nc.sync.dma_start(
                 out=x_in[j][:, first * K : last * K], in_=x_rows[:, (j * CHUNK + first) * K : (j * CHUNK + last) * K]
             )
 
-        def load_w(i):
-            w_tile = w_pool.tile([P, 4 * K], BF16, name="w_tile", tag="w_tile")
-            w_in[i] = w_tile
-            nc.sync.dma_start(out=w_tile[:], in_=w_rows[i])
+        def load_w(i, first=0, last=4):
+            if first == 0:
+                w_tile = w_pool.tile([P, 4 * K], BF16, name="w_tile", tag="w_tile")
+                w_in[i] = w_tile
+            cols = slice(first * K, last * K)
+            nc.sync.dma_start(out=w_in[i][:, cols], in_=w_rows[i][:, cols])
 
         def flip(source, half):
             words = source[:].bitcast(F32)
@@ -101,14 +107,26 @@ def tile_contractexpand_pa_kernel(tc, inputs_c_e, Ws, bs, out):
                 in_=bank[:].rearrange("q (t u p) -> q t p u", t=2, u=2),
             )
 
-        def unpack_w(i, half, bank):
+        def flip_w(i, half):
+            bank = flip(w_in[i], half)
+            if half == 0:
+                w_turned = wt_pool.tile([P, 4 * OUT], BF16, name="w_turned", tag="w_turned", align_bytes=64)
+                w_t[i] = w_turned
             nc.scalar.copy(
                 out=w_t[i][:].bitcast(F32).rearrange("q (p h m) -> q p h m", h=2, m=4)[:, :, half, :],
                 in_=bank[:].rearrange("q (m p) -> q p m", m=4),
             )
 
-        def flip_w(i, half):
-            unpack_w(i, half, flip(w_in[i], half))
+        def unpack_sum(dst, bank):
+            nc.scalar.copy(
+                out=dst[:].rearrange("q (p s) -> q p s", s=4), in_=bank[:].rearrange("q (s p) -> q p s", s=4)
+            )
+
+        def flip_sum(dst, source):
+            bank = flip_pool.tile([P, PSUM_BANK], F32, name="bank", tag="bank")
+            for s in range(4):
+                nc.tensor.transpose(bank[:, s * P : (s + 1) * P], source[:, s:K:4], identity[:])
+            unpack_sum(dst, bank)
 
         def spread_bias(i):
             spread = product_pool.tile([P, OUT], F32, name="spread", tag="product")
@@ -121,12 +139,26 @@ def tile_contractexpand_pa_kernel(tc, inputs_c_e, Ws, bs, out):
         def pool_copy(dst, src):
             nc.gpsimd.tensor_scalar(out=dst, in0=src, scalar1=1.0, scalar2=0.0, op0=MULT, op1=ADD)
 
-        def sum_pairs(j):
-            tiles = x_t[j][:].rearrange("q (g two n) -> q g two n", g=2, two=2)
-            add(pair_f32[j][:], tiles[:, :, 0, :], tiles[:, :, 1, :])
+        def pool_relu(i, dst, src):
+            nc.gpsimd.tensor_scalar(out=dst, in0=src, scalar1=0.0, scalar2=1.0 / GROUP[i], op0=MAX, op1=MULT)
 
-        def sum_quad(j, dst):
-            add(dst[:], pair_f32[j][:, 0, :], pair_f32[j][:, 1, :])
+        def sum_pair(j, g, count):
+            if j not in pair_f32:
+                pair = sum_pool.tile([P, 2, K], F32, name="pair", tag="pair")
+                pair_f32[j] = pair
+            tiles = x_in[j][:].rearrange("p (g two k) -> p g two k", g=2, two=2)[:, g : g + count, :, :]
+            add(pair_f32[j][:, g : g + count, :], tiles[:, :, 0, :], tiles[:, :, 1, :])
+
+        def sum_quad(j):
+            add(quad_f32[j][:], pair_f32[j][:, 0, :], pair_f32[j][:, 1, :])
+
+        def pair_up(j, engine):
+            pair = sum_pool.tile([P, 2 * K], BF16, name="pair_b", tag="pair_b", align_bytes=64)
+            pair_t[j] = pair
+            tiles = x_t[j][:].rearrange("q (g two n) -> q g two n", g=2, two=2)
+            engine.tensor_tensor(
+                out=pair[:].rearrange("q (g n) -> q g n", g=2), in0=tiles[:, :, 0, :], in1=tiles[:, :, 1, :], op=ADD
+            )
 
         def quantise(i, n, source):
             nc.vector.quantize_mx(out=codes[i][n][:].bitcast(FP8X4), scales=scales[i][n][:], in_=source[:])
@@ -152,117 +184,129 @@ def tile_contractexpand_pa_kernel(tc, inputs_c_e, Ws, bs, out):
         def add_bias(i, n, dst):
             add(dst, products[(i, n)][:], bias[:, i, :])
 
+        def add_bias_row(i, n):
+            row = row_pool.tile([P, 1, OUT], F32, name="row", tag="row")
+            single_rows[(i, n)] = row
+            add_bias(i, n, row[:, 0, :])
+
         def relu(i, dst, src):
             nc.scalar.activation(out=dst, in_=src, func=RELU, scale=1.0 / GROUP[i])
 
         def store(i, first, src):
             nc.sync.dma_start(out=out_rows[i, :, first : first + src.shape[1], :], in_=src)
 
-        def finish_row(i, first, row, cuts):
-            relu(i, row[:], row[:])
-            for count in cuts:
-                store(i, first, row[:].to_broadcast([P, count, OUT]))
-                first += count
+        def finish_group(i, n, copies):
+            if copies == 1:
+                rows = single_rows[(i, n)]
+            elif i == 3:
+                rows = ten_pool.tile([P, copies, OUT], F32, name="tens", tag="tens")
+            else:
+                rows = out_pool.tile([P, copies, OUT], F32, name="rows", tag="rows")
+            relu(i, rows[:], single_rows[(i, n)][:].to_broadcast([P, copies, OUT]))
+            for first in range(0, GROUP[i], copies):
+                store(i, n * GROUP[i] + first, rows[:])
 
-        def finish_quad(j):
-            rows = out_pool.tile([P, CHUNK, OUT], F32, name="rows", tag="rows")
-            relu(2, rows[:], quad_row[j][:].to_broadcast([P, CHUNK, OUT]))
-            store(2, j * CHUNK, rows[:])
+        def finish_ten_early(n):
+            row = single_rows[(3, n)]
+            relu(3, row[:], row[:])
+            store(3, n * GROUP[3], row[:].to_broadcast([P, 2, OUT]))
+            rows = ten_pool.tile([P, 2, OUT], F32, name="tens", tag="tens")
+            nc.scalar.copy(out=rows[:], in_=row[:].to_broadcast([P, 2, OUT]))
+            for first in range(2, GROUP[3], 2):
+                store(3, n * GROUP[3] + first, rows[:])
 
-        nc.vector.memset(bias_in[:], 0.0)
+        nc.vector.memset(bias_in[:].bitcast(F32), 0.0)
         nc.vector.memset(ones[:], 1.0)
         make_identity(nc, identity[:])
+        nc.scalar.dma_start(out=bias_in[0:1, :], in_=bias_row)
         load_x(0, 0, 2)
         load_x(0, 2, 4)
-        load_w(2)
+        load_w(2, 0, 2)
         load_x(1, 0, CHUNK)
-        load_x(2, 0, CHUNK)
-        nc.sync.dma_start(out=bias_in[0:1, :], in_=bias_row)
+        load_w(2, 2, 4)
+        load_x(2, 0, 2)
         load_w(3)
+        load_x(2, 2, 4)
         load_x(3, 0, CHUNK)
         load_x(4, 0, CHUNK)
-
-        flip_x(0, 0)
-        flip_x(0, 1)
-        flip_w(2, 0)
-        flip_w(2, 1)
         load_w(1)
-        sum_pairs(0)
-        sum_quad(0, quad_t[0])
-        quantise(2, 0, quad_t[0])
-        sum_quad(0, quad_f32[0])
-        quantise_w(2)
-        flip_x(1, 0)
-        flip_x(1, 1)
-        spread_bias(2)
-        flip_x(2, 0)
-        flip_x(2, 1)
-        multiply(2, 0)
-        sum_pairs(1)
-        sum_quad(1, quad_f32[1])
-        pool_copy(quad_t[1][:], quad_f32[1][:])
-        add_bias(2, 0, quad_row[0][:, 0, :])
-        flip_w(3, 0)
-        spread_bias(3)
-        last_bank = flip(w_in[3], 1)
+
+        sum_pair(0, 0, 1)
+        sum_pair(0, 1, 1)
+        sum_quad(0)
+        flip_w(2, 0)
+        flip_sum(quad_t[0], quad_f32[0])
+        flip_w(2, 1)
         load_w(0)
-        finish_row(2, 0, quad_row[0], (CHUNK,))
-        unpack_w(3, 1, last_bank)
+        spread_bias(2)
+        sum_pair(1, 0, 2)
+        sum_quad(1)
+        flip_sum(quad_t[1], quad_f32[1])
+        spread_bias(3)
+        flip_w(3, 0)
         add(eight_f32[0][:], quad_f32[0][:], quad_f32[1][:])
+        quantise_w(2)
+        quantise(2, 0, quad_t[0])
+        multiply(2, 0)
+        sum_pair(2, 0, 1)
+        add_bias_row(2, 0)
+        finish_group(2, 0, 1)
+        flip_w(3, 1)
         quantise(2, 1, quad_t[1])
-        flip_x(3, 0)
         multiply(2, 1)
-        flip_x(3, 1)
-        sum_pairs(2)
-        add_bias(2, 1, quad_row[1][:, 0, :])
-        finish_row(2, CHUNK, quad_row[1], (CHUNK,))
+        add(ten_f32[0][:], eight_f32[0][:], pair_f32[2][:, 0, :])
+        flip_sum(ten_t[0], ten_f32[0])
+        sum_pair(2, 1, 1)
+        add_bias_row(2, 1)
+        finish_group(2, 1, 1)
         quantise_w(3)
-        add(ten_t[0][:], eight_f32[0][:], pair_f32[2][:, 0, :])
         quantise(3, 0, ten_t[0])
-        sum_quad(2, quad_t[2])
-        quantise(2, 2, quad_t[2])
-        flip_x(4, 0)
-        flip_x(4, 1)
-        multiply(3, 0)
-        add_bias(3, 0, ten_row[0][:, 0, :])
-        finish_row(3, 0, ten_row[0], (4, 4, 2))
+        flip_x(0, 0)
         flip_w(1, 0)
-        multiply(2, 2)
+        multiply(3, 0)
+        sum_quad(2)
+        add_bias_row(3, 0)
+        finish_ten_early(0)
+        flip_sum(quad_t[2], quad_f32[2])
+        sum_pair(3, 0, 2)
+        sum_quad(3)
+        flip_sum(quad_t[3], quad_f32[3])
+        flip_x(0, 1)
         flip_w(1, 1)
-        flip_w(0, 0)
-        sum_pairs(3)
-        sum_quad(3, quad_f32[3])
-        pool_copy(quad_t[3][:], quad_f32[3][:])
-        add_bias(2, 2, quad_row[2][:, 0, :])
-        finish_quad(2)
-        sum_pairs(4)
+        add(eight_f32[1][:], pair_f32[2][:, 1, :], quad_f32[3][:])
+        sum_pair(4, 0, 2)
+        quantise(2, 2, quad_t[2])
+        multiply(2, 2)
+        spread_bias(1)
+        sum_quad(4)
         quantise(2, 3, quad_t[3])
         multiply(2, 3)
-        sum_quad(4, quad_f32[4])
-        pool_copy(quad_t[4][:], quad_f32[4][:])
-        add(eight_f32[1][:], pair_f32[2][:, 1, :], quad_f32[3][:])
-        add_bias(2, 3, quad_row[3][:, 0, :])
-        finish_quad(3)
-        add(ten_t[1][:], eight_f32[1][:], quad_f32[4][:])
-        quantise(3, 1, ten_t[1])
-        multiply(3, 1)
-        add_bias(3, 1, ten_row[1][:, 0, :])
-        relu(3, ten_rows[:], ten_row[1][:].to_broadcast([P, 5, OUT]))
-        store(3, 10, ten_rows[:])
-        store(3, 15, ten_rows[:])
-        flip_w(0, 1)
+        add_bias_row(2, 2)
+        finish_group(2, 2, 2)
+        flip_sum(quad_t[4], quad_f32[4])
+        add(ten_f32[1][:], eight_f32[1][:], quad_f32[4][:])
+        flip_sum(ten_t[1], ten_f32[1])
+        pair_up(0, nc.vector)
+        add_bias_row(2, 3)
+        flip_x(1, 0)
+        finish_group(2, 3, 2)
+        quantise_w(1)
         quantise(2, 4, quad_t[4])
         multiply(2, 4)
-        spread_bias(1)
-        spread_bias(0)
-        for j in range(CHUNKS):
-            pool_copy(pair_t[j][:], pair_f32[j][:].rearrange("q g n -> q (g n)"))
-        quantise_w(1)
-        quantise(0, 0, x_t[0])
+        quantise(3, 1, ten_t[1])
+        multiply(3, 1)
+        flip_w(0, 0)
         quantise(1, 0, pair_t[0])
-        add_bias(2, 4, quad_row[4][:, 0, :])
+        quantise(0, 0, x_t[0])
+        add_bias_row(3, 1)
+        finish_group(3, 1, 2)
+        add_bias_row(2, 4)
+        flip_w(0, 1)
+        flip_x(1, 1)
+        spread_bias(0)
         quantise_w(0)
-        finish_quad(4)
+        pair_up(1, nc.vector)
+        finish_group(2, 4, 2)
 
         passes = []
         for j in range(CHUNKS):
@@ -279,8 +323,12 @@ def tile_contractexpand_pa_kernel(tc, inputs_c_e, Ws, bs, out):
                 out_tiles[i] = rows
             rows = out_tiles[i]
             add_bias(i, n, rows[:, place * GROUP[i], :])
+            if place == 0 and j + 2 < CHUNKS:
+                flip_x(j + 2, 1 - i)
+            if i == 0 and place == CHUNK - 1 and j + 2 < CHUNKS:
+                pair_up(j + 2, nc.vector)
             if place == 1 and j + 1 < CHUNKS:
-                quantise(i, j + 1, (x_t, pair_t)[i][j + 1])
+                quantise(i, j + 1, x_t[j + 1] if i == 0 else pair_t[j + 1])
             if step + PRODUCT_BANKS < len(passes):
                 multiply(*passes[step + PRODUCT_BANKS])
             if i == 1 and place == 1:

@@ -30,6 +30,7 @@ def tile_contractexpand_pa_kernel(tc, inputs_c_e, Ws, bs, out):
     nc = tc.nc
     x_rows = inputs_c_e.rearrange("(p t) k -> p (t k)", t=TILES)
     w_rows = Ws.rearrange("i (p c) k -> i p (c k)", c=4)
+    w_halves = Ws.rearrange("i (h p c) k -> i h p (c k)", h=2, c=2)
     bias_row = bs.rearrange("(o i) d -> o (i d)", o=1)
     out_rows = out.rearrange("(i p t) d -> i p t d", i=len(GROUP), t=TILES)
 
@@ -81,12 +82,16 @@ def tile_contractexpand_pa_kernel(tc, inputs_c_e, Ws, bs, out):
                 out=x_in[j][:, first * K : last * K], in_=x_rows[:, (j * CHUNK + first) * K : (j * CHUNK + last) * K]
             )
 
-        def load_w(i, first=0, last=4):
-            if first == 0:
+        def load_w(i):
+            w_tile = w_pool.tile([P, 4 * K], BF16, name="w_tile", tag="w_tile")
+            w_in[i] = w_tile
+            nc.sync.dma_start(out=w_tile[:], in_=w_rows[i])
+
+        def load_w_half(i, half):
+            if half == 0:
                 w_tile = w_pool.tile([P, 4 * K], BF16, name="w_tile", tag="w_tile")
                 w_in[i] = w_tile
-            cols = slice(first * K, last * K)
-            nc.sync.dma_start(out=w_in[i][:, cols], in_=w_rows[i][:, cols])
+            nc.sync.dma_start(out=w_in[i][:, 2 * half * K : 2 * (half + 1) * K], in_=w_halves[i, half])
 
         def flip(source, half):
             words = source[:].bitcast(F32)
@@ -114,6 +119,16 @@ def tile_contractexpand_pa_kernel(tc, inputs_c_e, Ws, bs, out):
                 w_t[i] = w_turned
             nc.scalar.copy(
                 out=w_t[i][:].bitcast(F32).rearrange("q (p h m) -> q p h m", h=2, m=4)[:, :, half, :],
+                in_=bank[:].rearrange("q (m p) -> q p m", m=4),
+            )
+
+        def flip_w_half(i, half):
+            bank = flip(w_in[i], half)
+            if half == 0:
+                w_turned = wt_pool.tile([P, 4 * OUT], BF16, name="w_turned", tag="w_turned", align_bytes=64)
+                w_t[i] = w_turned
+            nc.scalar.copy(
+                out=w_t[i][:].bitcast(F32).rearrange("q (h p m) -> q h p m", h=2, m=4)[:, half, :, :],
                 in_=bank[:].rearrange("q (m p) -> q p m", m=4),
             )
 
@@ -166,6 +181,14 @@ def tile_contractexpand_pa_kernel(tc, inputs_c_e, Ws, bs, out):
         def quantise_w(i):
             nc.vector.quantize_mx(out=w_codes[i][:].bitcast(FP8X4), scales=w_scales[i][:], in_=w_t[i][:])
 
+        def quantise_w_half(i, half):
+            cols = slice(half * OUT // 2, (half + 1) * OUT // 2)
+            nc.vector.quantize_mx(
+                out=w_codes[i][:, cols].bitcast(FP8X4),
+                scales=w_scales[i][:, cols],
+                in_=w_t[i][:, 2 * half * OUT : 2 * (half + 1) * OUT],
+            )
+
         def multiply(i, n):
             per_tile = widths[i] // P
             cols = slice((n % per_tile) * P, (n % per_tile + 1) * P)
@@ -215,18 +238,19 @@ def tile_contractexpand_pa_kernel(tc, inputs_c_e, Ws, bs, out):
             for first in range(2, GROUP[3], 2):
                 store(3, n * GROUP[3] + first, rows[:])
 
-        nc.vector.memset(bias_in[:].bitcast(F32), 0.0)
+        nc.vector.memset(bias_in[:, 2 * OUT :].bitcast(F32), 0.0)
         nc.vector.memset(ones[:], 1.0)
+        nc.vector.memset(bias_in[:, : 2 * OUT].bitcast(F32), 0.0)
         make_identity(nc, identity[:])
-        nc.scalar.dma_start(out=bias_in[0:1, :], in_=bias_row)
         load_x(0, 0, 2)
         load_x(0, 2, 4)
-        load_w(2, 0, 2)
+        nc.sync.dma_start(out=bias_in[0:1, 2 * OUT :], in_=bias_row[:, 2 * OUT :])
+        load_w_half(2, 0)
         load_x(1, 0, CHUNK)
-        load_w(2, 2, 4)
-        load_x(2, 0, 2)
+        load_w_half(2, 1)
+        load_x(2, 0, CHUNK)
         load_w(3)
-        load_x(2, 2, 4)
+        nc.sync.dma_start(out=bias_in[0:1, : 2 * OUT], in_=bias_row[:, : 2 * OUT])
         load_x(3, 0, CHUNK)
         load_x(4, 0, CHUNK)
         load_w(1)
@@ -234,24 +258,25 @@ def tile_contractexpand_pa_kernel(tc, inputs_c_e, Ws, bs, out):
         sum_pair(0, 0, 1)
         sum_pair(0, 1, 1)
         sum_quad(0)
-        flip_w(2, 0)
-        flip_sum(quad_t[0], quad_f32[0])
-        flip_w(2, 1)
-        load_w(0)
         spread_bias(2)
+        spread_bias(3)
+        flip_w_half(2, 0)
+        flip_sum(quad_t[0], quad_f32[0])
+        flip_w_half(2, 1)
+        load_w(0)
         sum_pair(1, 0, 2)
         sum_quad(1)
         flip_sum(quad_t[1], quad_f32[1])
-        spread_bias(3)
-        flip_w(3, 0)
-        add(eight_f32[0][:], quad_f32[0][:], quad_f32[1][:])
-        quantise_w(2)
+        quantise_w_half(2, 0)
+        quantise_w_half(2, 1)
         quantise(2, 0, quad_t[0])
         multiply(2, 0)
         sum_pair(2, 0, 1)
         add_bias_row(2, 0)
         finish_group(2, 0, 1)
+        flip_w(3, 0)
         flip_w(3, 1)
+        add(eight_f32[0][:], quad_f32[0][:], quad_f32[1][:])
         quantise(2, 1, quad_t[1])
         multiply(2, 1)
         add(ten_f32[0][:], eight_f32[0][:], pair_f32[2][:, 0, :])
@@ -288,8 +313,8 @@ def tile_contractexpand_pa_kernel(tc, inputs_c_e, Ws, bs, out):
         flip_sum(ten_t[1], ten_f32[1])
         pair_up(0, nc.vector)
         add_bias_row(2, 3)
-        flip_x(1, 0)
         finish_group(2, 3, 2)
+        flip_x(1, 0)
         quantise_w(1)
         quantise(2, 4, quad_t[4])
         multiply(2, 4)

@@ -41,7 +41,8 @@ def tile_contractexpand_pa_kernel(tc, inputs_c_e, Ws, bs, out):
         sum_pool = ctx.enter_context(tc.tile_pool(name="sum_pool", bufs=3))
         row_pool = ctx.enter_context(tc.tile_pool(name="row_pool", bufs=3))
         ten_pool = ctx.enter_context(tc.tile_pool(name="ten_pool", bufs=2))
-        out_pool = ctx.enter_context(tc.tile_pool(name="out_pool", bufs=6))
+        out_pool = ctx.enter_context(tc.tile_pool(name="out_pool", bufs=5))
+        copies_pool = ctx.enter_context(tc.tile_pool(name="copies_pool", bufs=3))
         flip_pool = ctx.enter_context(tc.psum_pool(name="flip_pool", bufs=8 - PRODUCT_BANKS))
         product_pool = ctx.enter_context(tc.psum_pool(name="product_pool", bufs=PRODUCT_BANKS))
         ctx.enter_context(tc.manual_schedule())
@@ -218,25 +219,33 @@ def tile_contractexpand_pa_kernel(tc, inputs_c_e, Ws, bs, out):
         def store(i, first, src):
             nc.sync.dma_start(out=out_rows[i, :, first : first + src.shape[1], :], in_=src)
 
+        def store_copies(i, first, rows, times):
+            copies = rows[:].shape[2] // OUT
+            nc.sync.dma_start(
+                out=out_rows[i, :, first : first + times * copies, :].rearrange("p (t c) d -> p t (c d)", c=copies),
+                in_=rows[:].to_broadcast([P, times, copies * OUT]),
+            )
+
         def finish_group(i, n, copies):
+            row = single_rows[(i, n)]
             if copies == 1:
-                rows = single_rows[(i, n)]
-            elif i == 3:
-                rows = ten_pool.tile([P, copies, OUT], F32, name="tens", tag="tens")
+                rows = row
+                relu(i, row[:], row[:])
             else:
-                rows = out_pool.tile([P, copies, OUT], F32, name="rows", tag="rows")
-            relu(i, rows[:], single_rows[(i, n)][:].to_broadcast([P, copies, OUT]))
-            for first in range(0, GROUP[i], copies):
-                store(i, n * GROUP[i] + first, rows[:])
+                pool = ten_pool if i == 3 else copies_pool
+                rows = pool.tile([P, 1, copies * OUT], F32, name="copies", tag="copies")
+                relu(i, rows[:].rearrange("p o (c d) -> p (o c) d", c=copies), row[:].to_broadcast([P, copies, OUT]))
+            times = GROUP[i] // copies
+            for first in range(0, times, 4):
+                store_copies(i, n * GROUP[i] + first * copies, rows, min(4, times - first))
 
         def finish_ten_early(n):
             row = single_rows[(3, n)]
             relu(3, row[:], row[:])
-            store(3, n * GROUP[3], row[:].to_broadcast([P, 2, OUT]))
-            rows = ten_pool.tile([P, 2, OUT], F32, name="tens", tag="tens")
-            nc.scalar.copy(out=rows[:], in_=row[:].to_broadcast([P, 2, OUT]))
-            for first in range(2, GROUP[3], 2):
-                store(3, n * GROUP[3] + first, rows[:])
+            store_copies(3, n * GROUP[3], row, 2)
+            rows = ten_pool.tile([P, 1, 2 * OUT], F32, name="copies", tag="copies")
+            nc.scalar.copy(out=rows[:].rearrange("p o (c d) -> p (o c) d", c=2), in_=row[:].to_broadcast([P, 2, OUT]))
+            store_copies(3, n * GROUP[3] + 2, rows, 4)
 
         nc.vector.memset(bias_in[:, 2 * OUT :].bitcast(F32), 0.0)
         nc.vector.memset(ones[:], 1.0)

@@ -48,6 +48,7 @@ def tile_contractexpand_pa_kernel(tc, inputs_c_e, Ws, bs, out):
         ctx.enter_context(tc.manual_schedule())
 
         identity = keep.tile([P, P], F32, name="identity")
+        zeros = keep.tile([P, OUT], BF16, name="zeros")
         ones = keep.tile([P, P], BF16, name="ones")
         bias_in = keep.tile([P, len(GROUP) * OUT], BF16, name="bias_in")
         bias = keep.tile([P, len(GROUP), OUT], F32, name="bias")
@@ -143,6 +144,10 @@ def tile_contractexpand_pa_kernel(tc, inputs_c_e, Ws, bs, out):
             for s in range(4):
                 nc.tensor.transpose(bank[:, s * P : (s + 1) * P], source[:, s:K:4], identity[:])
             unpack_sum(dst, bank)
+
+        def keep_warm(count):
+            for n in range(count):
+                nc.tensor.matmul(out=unread[:], lhsT=ones[:], rhs=zeros[:], start=True, stop=True)
 
         def spread_bias(i):
             spread = product_pool.tile([P, OUT], F32, name="spread", tag="product")
@@ -249,6 +254,7 @@ def tile_contractexpand_pa_kernel(tc, inputs_c_e, Ws, bs, out):
 
         nc.vector.memset(bias_in[:, 2 * OUT :].bitcast(F32), 0.0)
         nc.vector.memset(ones[:], 1.0)
+        nc.vector.memset(zeros[:].bitcast(F32), 0.0)
         nc.vector.memset(bias_in[:, : 2 * OUT].bitcast(F32), 0.0)
         make_identity(nc, identity[:])
         load_x(0, 0, 2)
@@ -264,6 +270,8 @@ def tile_contractexpand_pa_kernel(tc, inputs_c_e, Ws, bs, out):
         load_x(4, 0, CHUNK)
         load_w(1)
 
+        unread = product_pool.tile([P, OUT], F32, name="unread", tag="product")
+        keep_warm(3)
         sum_pair(0, 0, 1)
         sum_pair(0, 1, 1)
         sum_quad(0)
@@ -272,6 +280,7 @@ def tile_contractexpand_pa_kernel(tc, inputs_c_e, Ws, bs, out):
         flip_w_half(2, 0)
         flip_sum(quad_t[0], quad_f32[0])
         flip_w_half(2, 1)
+        keep_warm(2)
         load_w(0)
         sum_pair(1, 0, 2)
         sum_quad(1)
@@ -280,6 +289,7 @@ def tile_contractexpand_pa_kernel(tc, inputs_c_e, Ws, bs, out):
         quantise_w_half(2, 1)
         quantise(2, 0, quad_t[0])
         multiply(2, 0)
+        keep_warm(2)
         sum_pair(2, 0, 1)
         add_bias_row(2, 0)
         finish_group(2, 0, 1)

@@ -61,7 +61,8 @@ def tile_contractexpand_pa_kernel(tc, inputs_c_e, Ws, bs, out):
         quad_f32 = [keep.tile([P, K], F32, name="quad_f32_%d" % j) for j in range(CHUNKS)]
         quad_t = [keep.tile([P, K], BF16, name="quad_t%d" % j, align_bytes=64) for j in range(CHUNKS)]
         eight_f32 = [keep.tile([P, K], F32, name="eight_f32_%d" % g) for g in range(2)]
-        ten_f32 = [keep.tile([P, K], F32, name="ten_f32_%d" % g) for g in range(2)]
+        quad_b = dict((j, keep.tile([P, K], BF16, name="quad_b%d" % j)) for j in (0, 2))
+        ten_b = [keep.tile([P, K], BF16, name="ten_b%d" % g) for g in range(2)]
         ten_t = [keep.tile([P, K], BF16, name="ten_t%d" % g, align_bytes=64) for g in range(2)]
         w_codes = [keep.tile([P, OUT], U32, name="w_codes%d" % i, align_bytes=64) for i in range(len(GROUP))]
         w_scales = [keep.tile([P, OUT], U8, name="w_scales%d" % i, align_bytes=64) for i in range(len(GROUP))]
@@ -139,6 +140,16 @@ def tile_contractexpand_pa_kernel(tc, inputs_c_e, Ws, bs, out):
                 out=dst[:].rearrange("q (p s) -> q p s", s=4), in_=bank[:].rearrange("q (s p) -> q p s", s=4)
             )
 
+        def flip_rounded(dst, source):
+            words = source[:].bitcast(F32)
+            bank = flip_pool.tile([P, PSUM_BANK], F32, name="bank", tag="bank")
+            for u in range(2):
+                nc.tensor.transpose(bank[:, u * P : (u + 1) * P], words[:, u : K // 2 : 2], identity[:])
+            nc.scalar.copy(
+                out=dst[:].bitcast(F32).rearrange("q (p u) -> q p u", u=2),
+                in_=bank[:, : 2 * P].rearrange("q (u p) -> q p u", u=2),
+            )
+
         def flip_sum(dst, source):
             bank = flip_pool.tile([P, PSUM_BANK], F32, name="bank", tag="bank")
             for s in range(4):
@@ -170,8 +181,8 @@ def tile_contractexpand_pa_kernel(tc, inputs_c_e, Ws, bs, out):
             tiles = x_in[j][:].rearrange("p (g two k) -> p g two k", g=2, two=2)[:, g : g + count, :, :]
             add(pair_f32[j][:, g : g + count, :], tiles[:, :, 0, :], tiles[:, :, 1, :])
 
-        def sum_quad(j):
-            add(quad_f32[j][:], pair_f32[j][:, 0, :], pair_f32[j][:, 1, :])
+        def sum_quad(j, dst):
+            add(dst[:], pair_f32[j][:, 0, :], pair_f32[j][:, 1, :])
 
         def pair_up(j, engine):
             pair = sum_pool.tile([P, 2 * K], BF16, name="pair_b", tag="pair_b", align_bytes=64)
@@ -274,81 +285,82 @@ def tile_contractexpand_pa_kernel(tc, inputs_c_e, Ws, bs, out):
         keep_warm(3)
         sum_pair(0, 0, 1)
         sum_pair(0, 1, 1)
-        sum_quad(0)
+        sum_quad(0, quad_b[0])
         spread_bias(2)
         spread_bias(3)
         flip_w_half(2, 0)
-        flip_sum(quad_t[0], quad_f32[0])
+        flip_rounded(quad_t[0], quad_b[0])
+        sum_quad(0, quad_f32[0])
         flip_w_half(2, 1)
         keep_warm(2)
         load_w(0)
         sum_pair(1, 0, 2)
-        sum_quad(1)
+        sum_quad(1, quad_f32[1])
         flip_sum(quad_t[1], quad_f32[1])
         quantise_w_half(2, 0)
-        quantise_w_half(2, 1)
         quantise(2, 0, quad_t[0])
+        quantise_w_half(2, 1)
         multiply(2, 0)
         keep_warm(2)
         sum_pair(2, 0, 1)
         add_bias_row(2, 0)
         finish_group(2, 0, 1)
-        flip_w(3, 0)
-        flip_w(3, 1)
-        add(eight_f32[0][:], quad_f32[0][:], quad_f32[1][:])
         quantise(2, 1, quad_t[1])
         multiply(2, 1)
-        add(ten_f32[0][:], eight_f32[0][:], pair_f32[2][:, 0, :])
-        flip_sum(ten_t[0], ten_f32[0])
+        flip_w(3, 0)
         sum_pair(2, 1, 1)
+        sum_quad(2, quad_b[2])
+        flip_rounded(quad_t[2], quad_b[2])
         add_bias_row(2, 1)
         finish_group(2, 1, 1)
-        quantise_w(3)
-        quantise(3, 0, ten_t[0])
-        flip_x(0, 0)
-        flip_w(1, 0)
-        multiply(3, 0)
-        sum_quad(2)
-        add_bias_row(3, 0)
-        finish_ten_early(0)
-        flip_sum(quad_t[2], quad_f32[2])
-        sum_pair(3, 0, 2)
-        sum_quad(3)
-        flip_sum(quad_t[3], quad_f32[3])
-        flip_x(0, 1)
-        flip_w(1, 1)
-        add(eight_f32[1][:], pair_f32[2][:, 1, :], quad_f32[3][:])
-        sum_pair(4, 0, 2)
+        flip_w(3, 1)
+        add(eight_f32[0][:], quad_f32[0][:], quad_f32[1][:])
         quantise(2, 2, quad_t[2])
         multiply(2, 2)
-        spread_bias(1)
-        sum_quad(4)
+        add(ten_b[0][:], eight_f32[0][:], pair_f32[2][:, 0, :])
+        flip_rounded(ten_t[0], ten_b[0])
+        add_bias_row(2, 2)
+        finish_group(2, 2, 1)
+        quantise_w(3)
+        flip_x(0, 0)
+        quantise(3, 0, ten_t[0])
+        multiply(3, 0)
+        sum_pair(3, 0, 2)
+        add_bias_row(3, 0)
+        finish_ten_early(0)
+        sum_quad(3, quad_f32[3])
+        flip_sum(quad_t[3], quad_f32[3])
+        flip_x(0, 1)
+        flip_w(1, 0)
+        sum_pair(4, 0, 2)
+        add(eight_f32[1][:], pair_f32[2][:, 1, :], quad_f32[3][:])
+        sum_quad(4, quad_f32[4])
         quantise(2, 3, quad_t[3])
         multiply(2, 3)
-        add_bias_row(2, 2)
-        finish_group(2, 2, 2)
-        flip_sum(quad_t[4], quad_f32[4])
-        add(ten_f32[1][:], eight_f32[1][:], quad_f32[4][:])
-        flip_sum(ten_t[1], ten_f32[1])
-        pair_up(0, nc.vector)
+        add(ten_b[1][:], eight_f32[1][:], quad_f32[4][:])
+        flip_rounded(ten_t[1], ten_b[1])
         add_bias_row(2, 3)
         finish_group(2, 3, 2)
-        flip_x(1, 0)
-        quantise_w(1)
-        quantise(2, 4, quad_t[4])
-        multiply(2, 4)
+        flip_sum(quad_t[4], quad_f32[4])
+        pair_up(0, nc.vector)
         quantise(3, 1, ten_t[1])
         multiply(3, 1)
-        flip_w(0, 0)
-        quantise(1, 0, pair_t[0])
-        quantise(0, 0, x_t[0])
+        flip_w(1, 1)
+        spread_bias(1)
+        quantise(2, 4, quad_t[4])
+        multiply(2, 4)
         add_bias_row(3, 1)
         finish_group(3, 1, 2)
+        flip_x(1, 0)
+        quantise(0, 0, x_t[0])
+        quantise_w(1)
         add_bias_row(2, 4)
+        flip_w(0, 0)
+        quantise(1, 0, pair_t[0])
         flip_w(0, 1)
         flip_x(1, 1)
-        spread_bias(0)
         quantise_w(0)
+        spread_bias(0)
         pair_up(1, nc.vector)
         finish_group(2, 4, 2)
 

@@ -52,7 +52,9 @@ def tile_contractexpand_pa_kernel(tc, inputs_c_e, Ws, bs, out):
         ones = keep.tile([P, P], BF16, name="ones")
         bias_in = keep.tile([P, len(GROUP) * OUT], BF16, name="bias_in")
         bias = keep.tile([P, len(GROUP), OUT], F32, name="bias")
-        x_in = [keep.tile([P, CHUNK * K], BF16, name="x_in%d" % j) for j in range(CHUNKS)]
+        x_in = [keep.tile([P, CHUNK * K], BF16, name="x_in%d" % j) for j in range(3)]
+        x_last = keep.tile([P, 2 * CHUNK * K], BF16, name="x_last")
+        x_in.extend(x_last[:, j * CHUNK * K : (j + 1) * CHUNK * K] for j in range(2))
         w_in = {}
         x_t = [keep.tile([P, CHUNK * K], BF16, name="x_t%d" % j, align_bytes=64) for j in range(CHUNKS)]
         w_t = {}
@@ -115,12 +117,12 @@ def tile_contractexpand_pa_kernel(tc, inputs_c_e, Ws, bs, out):
                 in_=bank[:].rearrange("q (t u p) -> q t p u", t=2, u=2),
             )
 
-        def flip_w(i, half):
+        def flip_w(i, half, copy=None):
             bank = flip(w_in[i], half)
             if half == 0:
                 w_turned = wt_pool.tile([P, 4 * OUT], BF16, name="w_turned", tag="w_turned", align_bytes=64)
                 w_t[i] = w_turned
-            nc.scalar.copy(
+            (copy or nc.scalar.copy)(
                 out=w_t[i][:].bitcast(F32).rearrange("q (p h m) -> q p h m", h=2, m=4)[:, :, half, :],
                 in_=bank[:].rearrange("q (m p) -> q p m", m=4),
             )
@@ -251,9 +253,25 @@ def tile_contractexpand_pa_kernel(tc, inputs_c_e, Ws, bs, out):
                 pool = ten_pool if i == 3 else copies_pool
                 rows = pool.tile([P, 1, copies * OUT], F32, name="copies", tag="copies")
                 relu(i, rows[:].rearrange("p o (c d) -> p (o c) d", c=copies), row[:].to_broadcast([P, copies, OUT]))
+            store_all(i, n, rows, copies)
+
+        def store_all(i, n, rows, copies):
             times = GROUP[i] // copies
             for first in range(0, times, 4):
                 store_copies(i, n * GROUP[i] + first * copies, rows, min(4, times - first))
+            if GROUP[i] % copies:
+                left = GROUP[i] % copies
+                nc.sync.dma_start(
+                    out=out_rows[i, :, (n + 1) * GROUP[i] - left : (n + 1) * GROUP[i], :].rearrange("p (o c) d -> p o (c d)", o=1),
+                    in_=rows[:, :, : left * OUT],
+                )
+
+        def finish_with_pool(i, n, copies):
+            rows = (ten_pool if i == 3 else copies_pool).tile([P, 1, copies * OUT], F32, name="copies", tag="copies")
+            each = rows[:].rearrange("p o (c d) -> p (o c) d", c=copies)
+            relu(i, each[:, 0:1, :], single_rows[(i, n)][:])
+            pool_copy(each[:, 1:copies, :], each[:, 0:1, :].to_broadcast([P, copies - 1, OUT]))
+            store_all(i, n, rows, copies)
 
         def finish_ten_early(n):
             row = single_rows[(3, n)]
@@ -277,8 +295,7 @@ def tile_contractexpand_pa_kernel(tc, inputs_c_e, Ws, bs, out):
         load_x(2, 0, CHUNK)
         load_w(3)
         nc.sync.dma_start(out=bias_in[0:1, : 2 * OUT], in_=bias_row[:, : 2 * OUT])
-        load_x(3, 0, CHUNK)
-        load_x(4, 0, CHUNK)
+        nc.sync.dma_start(out=x_last[:], in_=x_rows[:, 3 * CHUNK * K :])
         load_w(1)
 
         unread = product_pool.tile([P, OUT], F32, name="unread", tag="product")
@@ -327,7 +344,7 @@ def tile_contractexpand_pa_kernel(tc, inputs_c_e, Ws, bs, out):
         multiply(3, 0)
         sum_pair(3, 0, 2)
         add_bias_row(3, 0)
-        finish_ten_early(0)
+        finish_group(3, 0, 2)
         sum_quad(3, quad_f32[3])
         flip_sum(quad_t[3], quad_f32[3])
         flip_x(0, 1)
@@ -340,7 +357,7 @@ def tile_contractexpand_pa_kernel(tc, inputs_c_e, Ws, bs, out):
         add(ten_b[1][:], eight_f32[1][:], quad_f32[4][:])
         flip_rounded(ten_t[1], ten_b[1])
         add_bias_row(2, 3)
-        finish_group(2, 3, 2)
+        finish_with_pool(2, 3, 2)
         flip_sum(quad_t[4], quad_f32[4])
         pair_up(0, nc.vector)
         quantise(3, 1, ten_t[1])
@@ -350,19 +367,19 @@ def tile_contractexpand_pa_kernel(tc, inputs_c_e, Ws, bs, out):
         quantise(2, 4, quad_t[4])
         multiply(2, 4)
         add_bias_row(3, 1)
-        finish_group(3, 1, 2)
+        finish_with_pool(3, 1, 2)
         flip_x(1, 0)
         quantise(0, 0, x_t[0])
         quantise_w(1)
         add_bias_row(2, 4)
         flip_w(0, 0)
         quantise(1, 0, pair_t[0])
-        flip_w(0, 1)
+        flip_w(0, 1, nc.vector.tensor_copy)
         flip_x(1, 1)
         quantise_w(0)
         spread_bias(0)
         pair_up(1, nc.vector)
-        finish_group(2, 4, 2)
+        finish_with_pool(2, 4, 4)
 
         passes = []
         for j in range(CHUNKS):

@@ -292,9 +292,9 @@ def tile_contractexpand_pa_kernel(tc, inputs_c_e, Ws, bs, out):
         load_w_half(2, 0)
         load_x(1, 0, CHUNK)
         load_w_half(2, 1)
+        nc.sync.dma_start(out=bias_in[0:1, : 2 * OUT], in_=bias_row[:, : 2 * OUT])
         load_x(2, 0, CHUNK)
         load_w(3)
-        nc.sync.dma_start(out=bias_in[0:1, : 2 * OUT], in_=bias_row[:, : 2 * OUT])
         nc.sync.dma_start(out=x_last[:], in_=x_rows[:, 3 * CHUNK * K :])
         load_w(1)
 
@@ -309,7 +309,7 @@ def tile_contractexpand_pa_kernel(tc, inputs_c_e, Ws, bs, out):
         flip_rounded(quad_t[0], quad_b[0])
         sum_quad(0, quad_f32[0])
         flip_w_half(2, 1)
-        keep_warm(2)
+        spread_bias(1)
         load_w(0)
         sum_pair(1, 0, 2)
         sum_quad(1, quad_f32[1])
@@ -322,6 +322,7 @@ def tile_contractexpand_pa_kernel(tc, inputs_c_e, Ws, bs, out):
         sum_pair(2, 0, 1)
         add_bias_row(2, 0)
         finish_group(2, 0, 1)
+        spread_bias(0)
         quantise(2, 1, quad_t[1])
         multiply(2, 1)
         flip_w(3, 0)
@@ -340,6 +341,7 @@ def tile_contractexpand_pa_kernel(tc, inputs_c_e, Ws, bs, out):
         finish_group(2, 2, 1)
         quantise_w(3)
         flip_x(0, 0)
+        flip_w(1, 0)
         quantise(3, 0, ten_t[0])
         multiply(3, 0)
         sum_pair(3, 0, 2)
@@ -348,7 +350,7 @@ def tile_contractexpand_pa_kernel(tc, inputs_c_e, Ws, bs, out):
         sum_quad(3, quad_f32[3])
         flip_sum(quad_t[3], quad_f32[3])
         flip_x(0, 1)
-        flip_w(1, 0)
+        flip_w(1, 1)
         sum_pair(4, 0, 2)
         add(eight_f32[1][:], pair_f32[2][:, 1, :], quad_f32[3][:])
         sum_quad(4, quad_f32[4])
@@ -357,29 +359,26 @@ def tile_contractexpand_pa_kernel(tc, inputs_c_e, Ws, bs, out):
         add(ten_b[1][:], eight_f32[1][:], quad_f32[4][:])
         flip_rounded(ten_t[1], ten_b[1])
         add_bias_row(2, 3)
-        finish_with_pool(2, 3, 2)
+        finish_group(2, 3, 1)
         flip_sum(quad_t[4], quad_f32[4])
         pair_up(0, nc.vector)
         quantise(3, 1, ten_t[1])
         multiply(3, 1)
-        flip_w(1, 1)
-        spread_bias(1)
+        quantise_w(1)
+        flip_w(0, 0)
         quantise(2, 4, quad_t[4])
         multiply(2, 4)
         add_bias_row(3, 1)
-        finish_with_pool(3, 1, 2)
+        finish_group(3, 1, 1)
         flip_x(1, 0)
-        quantise(0, 0, x_t[0])
-        quantise_w(1)
-        add_bias_row(2, 4)
-        flip_w(0, 0)
         quantise(1, 0, pair_t[0])
-        flip_w(0, 1, nc.vector.tensor_copy)
+        quantise(0, 0, x_t[0])
         flip_x(1, 1)
-        quantise_w(0)
-        spread_bias(0)
+        add_bias_row(2, 4)
+        flip_w(0, 1)
         pair_up(1, nc.vector)
-        finish_with_pool(2, 4, 4)
+        quantise_w(0)
+        finish_group(2, 4, 2)
 
         passes = []
         for j in range(CHUNKS):

@@ -41,7 +41,7 @@ def tile_contractexpand_pa_kernel(tc, inputs_c_e, Ws, bs, out):
         sum_pool = ctx.enter_context(tc.tile_pool(name="sum_pool", bufs=3))
         row_pool = ctx.enter_context(tc.tile_pool(name="row_pool", bufs=3))
         ten_pool = ctx.enter_context(tc.tile_pool(name="ten_pool", bufs=2))
-        out_pool = ctx.enter_context(tc.tile_pool(name="out_pool", bufs=5))
+        out_pool = ctx.enter_context(tc.tile_pool(name="out_pool", bufs=6))
         copies_pool = ctx.enter_context(tc.tile_pool(name="copies_pool", bufs=3))
         flip_pool = ctx.enter_context(tc.psum_pool(name="flip_pool", bufs=8 - PRODUCT_BANKS))
         product_pool = ctx.enter_context(tc.psum_pool(name="product_pool", bufs=PRODUCT_BANKS))
@@ -346,7 +346,7 @@ def tile_contractexpand_pa_kernel(tc, inputs_c_e, Ws, bs, out):
         multiply(3, 0)
         sum_pair(3, 0, 2)
         add_bias_row(3, 0)
-        finish_group(3, 0, 2)
+        finish_ten_early(0)
         sum_quad(3, quad_f32[3])
         flip_sum(quad_t[3], quad_f32[3])
         flip_x(0, 1)
@@ -361,16 +361,16 @@ def tile_contractexpand_pa_kernel(tc, inputs_c_e, Ws, bs, out):
         add_bias_row(2, 3)
         finish_group(2, 3, 1)
         flip_sum(quad_t[4], quad_f32[4])
+        flip_w(0, 0)
         pair_up(0, nc.vector)
         quantise(3, 1, ten_t[1])
         multiply(3, 1)
+        flip_x(1, 0)
         quantise_w(1)
-        flip_w(0, 0)
         quantise(2, 4, quad_t[4])
         multiply(2, 4)
         add_bias_row(3, 1)
-        finish_group(3, 1, 1)
-        flip_x(1, 0)
+        finish_group(3, 1, 2)
         quantise(1, 0, pair_t[0])
         quantise(0, 0, x_t[0])
         flip_x(1, 1)
@@ -379,6 +379,8 @@ def tile_contractexpand_pa_kernel(tc, inputs_c_e, Ws, bs, out):
         pair_up(1, nc.vector)
         quantise_w(0)
         finish_group(2, 4, 2)
+        flip_x(2, 0)
+        flip_x(2, 1)
 
         passes = []
         for j in range(CHUNKS):
@@ -395,9 +397,9 @@ def tile_contractexpand_pa_kernel(tc, inputs_c_e, Ws, bs, out):
                 out_tiles[i] = rows
             rows = out_tiles[i]
             add_bias(i, n, rows[:, place * GROUP[i], :])
-            if place == 0 and j + 2 < CHUNKS:
-                flip_x(j + 2, 1 - i)
-            if i == 0 and place == CHUNK - 1 and j + 2 < CHUNKS:
+            if place == 0 and j + 3 < CHUNKS:
+                flip_x(j + 3, 1 - i)
+            if i == 0 and place == 0 and j + 2 < CHUNKS:
                 pair_up(j + 2, nc.vector)
             if place == 1 and j + 1 < CHUNKS:
                 quantise(i, j + 1, x_t[j + 1] if i == 0 else pair_t[j + 1])

from contextlib import ExitStack

import concourse.mybir as mybir
from concourse.masks import make_identity

F32 = mybir.dt.float32
BF16 = mybir.dt.bfloat16
U32 = mybir.dt.uint32
U8 = mybir.dt.uint8
FP8X4 = mybir.dt.float8_e4m3fn_x4
ADD = mybir.AluOpType.add
MAX = mybir.AluOpType.max
MULT = mybir.AluOpType.mult
RELU = mybir.ActivationFunctionType.Relu

P = 128
ROWS = 2560
K = 512
OUT = 512
GROUP = (1, 2, 4, 10)
TILES = ROWS // P
CHUNK = 4
CHUNKS = TILES // CHUNK
PSUM_BANK = 512
PRODUCT_BANKS = 5
FLOPS = 2 * sum(ROWS // r for r in GROUP) * K * OUT


def tile_contractexpand_pa_kernel(tc, inputs_c_e, Ws, bs, out):
    nc = tc.nc
    x_rows = inputs_c_e.rearrange("(p t) k -> p (t k)", t=TILES)
    w_rows = Ws.rearrange("i (p c) k -> i p (c k)", c=4)
    w_halves = Ws.rearrange("i (h p c) k -> i h p (c k)", h=2, c=2)
    bias_row = bs.rearrange("(o i) d -> o (i d)", o=1)
    out_rows = out.rearrange("(i p t) d -> i p t d", i=len(GROUP), t=TILES)

    with ExitStack() as ctx:
        keep = ctx.enter_context(tc.tile_pool(name="keep", bufs=1))
        w_pool = ctx.enter_context(tc.tile_pool(name="w_pool", bufs=3))
        wt_pool = ctx.enter_context(tc.tile_pool(name="wt_pool", bufs=2))
        sum_pool = ctx.enter_context(tc.tile_pool(name="sum_pool", bufs=3))
        row_pool = ctx.enter_context(tc.tile_pool(name="row_pool", bufs=3))
        ten_pool = ctx.enter_context(tc.tile_pool(name="ten_pool", bufs=2))
        out_pool = ctx.enter_context(tc.tile_pool(name="out_pool", bufs=6))
        copies_pool = ctx.enter_context(tc.tile_pool(name="copies_pool", bufs=3))
        flip_pool = ctx.enter_context(tc.psum_pool(name="flip_pool", bufs=8 - PRODUCT_BANKS))
        product_pool = ctx.enter_context(tc.psum_pool(name="product_pool", bufs=PRODUCT_BANKS))
        ctx.enter_context(tc.manual_schedule())

        identity = keep.tile([P, P], F32, name="identity")
        zeros = keep.tile([P, OUT], BF16, name="zeros")
        ones = keep.tile([P, P], BF16, name="ones")
        bias_in = keep.tile([P, len(GROUP) * OUT], BF16, name="bias_in")
        bias = keep.tile([P, len(GROUP), OUT], F32, name="bias")
        x_in = [keep.tile([P, CHUNK * K], BF16, name="x_in%d" % j) for j in range(3)]
        x_last = keep.tile([P, 2 * CHUNK * K], BF16, name="x_last")
        x_in.extend(x_last[:, j * CHUNK * K : (j + 1) * CHUNK * K] for j in range(2))
        w_in = {}
        x_t = [keep.tile([P, CHUNK * K], BF16, name="x_t%d" % j, align_bytes=64) for j in range(CHUNKS)]
        w_t = {}
        pair_t = {}
        pair_f32 = {}
        quad_f32 = [keep.tile([P, K], F32, name="quad_f32_%d" % j) for j in range(CHUNKS)]
        quad_t = [keep.tile([P, K], BF16, name="quad_t%d" % j, align_bytes=64) for j in range(CHUNKS)]
        eight_f32 = [keep.tile([P, K], F32, name="eight_f32_%d" % g) for g in range(2)]
        quad_b = dict((j, keep.tile([P, K], BF16, name="quad_b%d" % j)) for j in (0, 2))
        ten_b = [keep.tile([P, K], BF16, name="ten_b%d" % g) for g in range(2)]
        ten_t = [keep.tile([P, K], BF16, name="ten_t%d" % g, align_bytes=64) for g in range(2)]
        w_codes = [keep.tile([P, OUT], U32, name="w_codes%d" % i, align_bytes=64) for i in range(len(GROUP))]
        w_scales = [keep.tile([P, OUT], U8, name="w_scales%d" % i, align_bytes=64) for i in range(len(GROUP))]
        widths = (CHUNK * P, 2 * P, P, P)
        counts = (CHUNKS, CHUNKS, CHUNKS, 2)
        codes = [
            [keep.tile([P, widths[i]], U32, name="codes%d_%d" % (i, n), align_bytes=64) for n in range(counts[i])]
            for i in range(len(GROUP))
        ]
        scales = [
            [keep.tile([P, widths[i]], U8, name="scales%d_%d" % (i, n), align_bytes=64) for n in range(counts[i])]
            for i in range(len(GROUP))
        ]
        products = {}
        out_tiles = {}
        single_rows = {}

        def load_x(j, first, last):
            nc.sync.dma_start(
                out=x_in[j][:, first * K : last * K], in_=x_rows[:, (j * CHUNK + first) * K : (j * CHUNK + last) * K]
            )

        def load_w(i):
            w_tile = w_pool.tile([P, 4 * K], BF16, name="w_tile", tag="w_tile")
            w_in[i] = w_tile
            nc.sync.dma_start(out=w_tile[:], in_=w_rows[i])

        def load_w_half(i, half):
            if half == 0:
                w_tile = w_pool.tile([P, 4 * K], BF16, name="w_tile", tag="w_tile")
                w_in[i] = w_tile
            nc.sync.dma_start(out=w_in[i][:, 2 * half * K : 2 * (half + 1) * K], in_=w_halves[i, half])

        def flip(source, half):
            words = source[:].bitcast(F32)
            bank = flip_pool.tile([P, PSUM_BANK], F32, name="bank", tag="bank")
            for m in range(4):
                first = (2 * half + m // 2) * (K // 2)
                nc.tensor.transpose(
                    bank[:, m * P : (m + 1) * P], words[:, first + m % 2 : first + K // 2 : 2], identity[:]
                )
            return bank

        def flip_x(j, half):
            bank = flip(x_in[j], half)
            nc.scalar.copy(
                out=x_t[j][:].bitcast(F32).rearrange("q (t p u) -> q t p u", t=CHUNK, u=2)[
                    :, 2 * half : 2 * half + 2, :, :
                ],
                in_=bank[:].rearrange("q (t u p) -> q t p u", t=2, u=2),
            )

        def flip_w(i, half, copy=None):
            bank = flip(w_in[i], half)
            if half == 0:
                w_turned = wt_pool.tile([P, 4 * OUT], BF16, name="w_turned", tag="w_turned", align_bytes=64)
                w_t[i] = w_turned
            (copy or nc.scalar.copy)(
                out=w_t[i][:].bitcast(F32).rearrange("q (p h m) -> q p h m", h=2, m=4)[:, :, half, :],
                in_=bank[:].rearrange("q (m p) -> q p m", m=4),
            )

        def flip_w_half(i, half):
            bank = flip(w_in[i], half)
            if half == 0:
                w_turned = wt_pool.tile([P, 4 * OUT], BF16, name="w_turned", tag="w_turned", align_bytes=64)
                w_t[i] = w_turned
            nc.scalar.copy(
                out=w_t[i][:].bitcast(F32).rearrange("q (h p m) -> q h p m", h=2, m=4)[:, half, :, :],
                in_=bank[:].rearrange("q (m p) -> q p m", m=4),
            )

        def unpack_sum(dst, bank):
            nc.scalar.copy(
                out=dst[:].rearrange("q (p s) -> q p s", s=4), in_=bank[:].rearrange("q (s p) -> q p s", s=4)
            )

        def flip_rounded(dst, source):
            words = source[:].bitcast(F32)
            bank = flip_pool.tile([P, PSUM_BANK], F32, name="bank", tag="bank")
            for u in range(2):
                nc.tensor.transpose(bank[:, u * P : (u + 1) * P], words[:, u : K // 2 : 2], identity[:])
            nc.scalar.copy(
                out=dst[:].bitcast(F32).rearrange("q (p u) -> q p u", u=2),
                in_=bank[:, : 2 * P].rearrange("q (u p) -> q p u", u=2),
            )

        def flip_sum(dst, source):
            bank = flip_pool.tile([P, PSUM_BANK], F32, name="bank", tag="bank")
            for s in range(4):
                nc.tensor.transpose(bank[:, s * P : (s + 1) * P], source[:, s:K:4], identity[:])
            unpack_sum(dst, bank)

        def keep_warm(count):
            for n in range(count):
                nc.tensor.matmul(out=unread[:], lhsT=ones[:], rhs=zeros[:], start=True, stop=True)

        def spread_bias(i):
            spread = product_pool.tile([P, OUT], F32, name="spread", tag="product")
            nc.tensor.matmul(out=spread[:], lhsT=ones[:], rhs=bias_in[:, i * OUT : (i + 1) * OUT], start=True, stop=True)
            nc.scalar.copy(out=bias[:, i, :], in_=spread[:])

        def add(dst, a, b):
            nc.vector.tensor_tensor(out=dst, in0=a, in1=b, op=ADD)

        def pool_copy(dst, src):
            nc.gpsimd.tensor_scalar(out=dst, in0=src, scalar1=1.0, scalar2=0.0, op0=MULT, op1=ADD)

        def pool_relu(i, dst, src):
            nc.gpsimd.tensor_scalar(out=dst, in0=src, scalar1=0.0, scalar2=1.0 / GROUP[i], op0=MAX, op1=MULT)

        def sum_pair(j, g, count):
            if j not in pair_f32:
                pair = sum_pool.tile([P, 2, K], F32, name="pair", tag="pair")
                pair_f32[j] = pair
            tiles = x_in[j][:].rearrange("p (g two k) -> p g two k", g=2, two=2)[:, g : g + count, :, :]
            add(pair_f32[j][:, g : g + count, :], tiles[:, :, 0, :], tiles[:, :, 1, :])

        def sum_quad(j, dst):
            add(dst[:], pair_f32[j][:, 0, :], pair_f32[j][:, 1, :])

        def pair_up(j, engine):
            pair = sum_pool.tile([P, 2 * K], BF16, name="pair_b", tag="pair_b", align_bytes=64)
            pair_t[j] = pair
            tiles = x_t[j][:].rearrange("q (g two n) -> q g two n", g=2, two=2)
            engine.tensor_tensor(
                out=pair[:].rearrange("q (g n) -> q g n", g=2), in0=tiles[:, :, 0, :], in1=tiles[:, :, 1, :], op=ADD
            )

        def quantise(i, n, source):
            nc.vector.quantize_mx(out=codes[i][n][:].bitcast(FP8X4), scales=scales[i][n][:], in_=source[:])

        def quantise_w(i):
            nc.vector.quantize_mx(out=w_codes[i][:].bitcast(FP8X4), scales=w_scales[i][:], in_=w_t[i][:])

        def quantise_w_half(i, half):
            cols = slice(half * OUT // 2, (half + 1) * OUT // 2)
            nc.vector.quantize_mx(
                out=w_codes[i][:, cols].bitcast(FP8X4),
                scales=w_scales[i][:, cols],
                in_=w_t[i][:, 2 * half * OUT : 2 * (half + 1) * OUT],
            )

        def multiply(i, n):
            per_tile = widths[i] // P
            cols = slice((n % per_tile) * P, (n % per_tile + 1) * P)
            product = product_pool.tile([P, OUT], F32, name="product", tag="product")
            products[(i, n)] = product
            nc.tensor.matmul_mx(
                out=product[:],
                lhsT=codes[i][n // per_tile][:, cols].bitcast(FP8X4),
                lhsT_scale=scales[i][n // per_tile][:, cols],
                rhs=w_codes[i][:].bitcast(FP8X4),
                rhs_scale=w_scales[i][:],
                start=True,
                stop=True,
            )

        def add_bias(i, n, dst):
            add(dst, products[(i, n)][:], bias[:, i, :])

        def add_bias_row(i, n):
            row = row_pool.tile([P, 1, OUT], F32, name="row", tag="row")
            single_rows[(i, n)] = row
            add_bias(i, n, row[:, 0, :])

        def relu(i, dst, src):
            nc.scalar.activation(out=dst, in_=src, func=RELU, scale=1.0 / GROUP[i])

        def store(i, first, src):
            nc.sync.dma_start(out=out_rows[i, :, first : first + src.shape[1], :], in_=src)

        def store_copies(i, first, rows, times):
            copies = rows[:].shape[2] // OUT
            nc.sync.dma_start(
                out=out_rows[i, :, first : first + times * copies, :].rearrange("p (t c) d -> p t (c d)", c=copies),
                in_=rows[:].to_broadcast([P, times, copies * OUT]),
            )

        def finish_group(i, n, copies):
            row = single_rows[(i, n)]
            if copies == 1:
                rows = row
                relu(i, row[:], row[:])
            else:
                pool = ten_pool if i == 3 else copies_pool
                rows = pool.tile([P, 1, copies * OUT], F32, name="copies", tag="copies")
                relu(i, rows[:].rearrange("p o (c d) -> p (o c) d", c=copies), row[:].to_broadcast([P, copies, OUT]))
            store_all(i, n, rows, copies)

        def store_all(i, n, rows, copies):
            times = GROUP[i] // copies
            for first in range(0, times, 4):
                store_copies(i, n * GROUP[i] + first * copies, rows, min(4, times - first))
            if GROUP[i] % copies:
                left = GROUP[i] % copies
                nc.sync.dma_start(
                    out=out_rows[i, :, (n + 1) * GROUP[i] - left : (n + 1) * GROUP[i], :].rearrange("p (o c) d -> p o (c d)", o=1),
                    in_=rows[:, :, : left * OUT],
                )

        def finish_with_pool(i, n, copies):
            rows = (ten_pool if i == 3 else copies_pool).tile([P, 1, copies * OUT], F32, name="copies", tag="copies")
            each = rows[:].rearrange("p o (c d) -> p (o c) d", c=copies)
            relu(i, each[:, 0:1, :], single_rows[(i, n)][:])
            pool_copy(each[:, 1:copies, :], each[:, 0:1, :].to_broadcast([P, copies - 1, OUT]))
            store_all(i, n, rows, copies)

        def finish_ten_early(n):
            row = single_rows[(3, n)]
            relu(3, row[:], row[:])
            store_copies(3, n * GROUP[3], row, 2)
            rows = ten_pool.tile([P, 1, 2 * OUT], F32, name="copies", tag="copies")
            nc.scalar.copy(out=rows[:].rearrange("p o (c d) -> p (o c) d", c=2), in_=row[:].to_broadcast([P, 2, OUT]))
            store_copies(3, n * GROUP[3] + 2, rows, 4)

        nc.vector.memset(bias_in[:, 2 * OUT :].bitcast(F32), 0.0)
        nc.vector.memset(ones[:], 1.0)
        nc.vector.memset(zeros[:].bitcast(F32), 0.0)
        nc.vector.memset(bias_in[:, : 2 * OUT].bitcast(F32), 0.0)
        make_identity(nc, identity[:])
        load_x(0, 0, 2)
        load_x(0, 2, 4)
        nc.sync.dma_start(out=bias_in[0:1, 2 * OUT :], in_=bias_row[:, 2 * OUT :])
        load_w_half(2, 0)
        load_x(1, 0, CHUNK)
        load_w_half(2, 1)
        nc.sync.dma_start(out=bias_in[0:1, : 2 * OUT], in_=bias_row[:, : 2 * OUT])
        load_x(2, 0, CHUNK)
        load_w(3)
        nc.sync.dma_start(out=x_last[:], in_=x_rows[:, 3 * CHUNK * K :])
        load_w(1)

        unread = product_pool.tile([P, OUT], F32, name="unread", tag="product")
        keep_warm(3)
        sum_pair(0, 0, 1)
        sum_pair(0, 1, 1)
        sum_quad(0, quad_b[0])
        spread_bias(2)
        spread_bias(3)
        flip_w_half(2, 0)
        flip_rounded(quad_t[0], quad_b[0])
        sum_quad(0, quad_f32[0])
        flip_w_half(2, 1)
        spread_bias(1)
        load_w(0)
        sum_pair(1, 0, 2)
        sum_quad(1, quad_f32[1])
        flip_sum(quad_t[1], quad_f32[1])
        quantise_w_half(2, 0)
        quantise(2, 0, quad_t[0])
        quantise_w_half(2, 1)
        multiply(2, 0)
        keep_warm(2)
        sum_pair(2, 0, 1)
        add_bias_row(2, 0)
        finish_group(2, 0, 1)
        spread_bias(0)
        quantise(2, 1, quad_t[1])
        multiply(2, 1)
        flip_w(3, 0)
        sum_pair(2, 1, 1)
        sum_quad(2, quad_b[2])
        flip_rounded(quad_t[2], quad_b[2])
        add_bias_row(2, 1)
        finish_group(2, 1, 1)
        flip_w(3, 1)
        add(eight_f32[0][:], quad_f32[0][:], quad_f32[1][:])
        quantise(2, 2, quad_t[2])
        multiply(2, 2)
        add(ten_b[0][:], eight_f32[0][:], pair_f32[2][:, 0, :])
        flip_rounded(ten_t[0], ten_b[0])
        add_bias_row(2, 2)
        finish_group(2, 2, 1)
        quantise_w(3)
        flip_x(0, 0)
        flip_w(1, 0)
        quantise(3, 0, ten_t[0])
        multiply(3, 0)
        sum_pair(3, 0, 2)
        add_bias_row(3, 0)
        finish_ten_early(0)
        sum_quad(3, quad_f32[3])
        flip_sum(quad_t[3], quad_f32[3])
        flip_x(0, 1)
        flip_w(1, 1)
        sum_pair(4, 0, 2)
        add(eight_f32[1][:], pair_f32[2][:, 1, :], quad_f32[3][:])
        sum_quad(4, quad_f32[4])
        quantise(2, 3, quad_t[3])
        multiply(2, 3)
        add(ten_b[1][:], eight_f32[1][:], quad_f32[4][:])
        flip_rounded(ten_t[1], ten_b[1])
        add_bias_row(2, 3)
        finish_group(2, 3, 1)
        flip_sum(quad_t[4], quad_f32[4])
        flip_w(0, 0)
        pair_up(0, nc.vector)
        quantise(3, 1, ten_t[1])
        multiply(3, 1)
        flip_x(1, 0)
        quantise_w(1)
        quantise(2, 4, quad_t[4])
        multiply(2, 4)
        add_bias_row(3, 1)
        finish_group(3, 1, 2)
        quantise(1, 0, pair_t[0])
        quantise(0, 0, x_t[0])
        flip_x(1, 1)
        add_bias_row(2, 4)
        flip_w(0, 1)
        pair_up(1, nc.vector)
        quantise_w(0)
        finish_group(2, 4, 2)
        flip_x(2, 0)
        flip_x(2, 1)

        passes = []
        for j in range(CHUNKS):
            passes.extend((1, 2 * j + g) for g in range(2))
            passes.extend((0, CHUNK * j + t) for t in range(CHUNK))
        for i, n in passes[:PRODUCT_BANKS]:
            multiply(i, n)
        for step, (i, n) in enumerate(passes):
            per_chunk = CHUNK // GROUP[i]
            j = n // per_chunk
            place = n % per_chunk
            if place == 0:
                rows = out_pool.tile([P, CHUNK, OUT], F32, name="rows", tag="rows")
                out_tiles[i] = rows
            rows = out_tiles[i]
            add_bias(i, n, rows[:, place * GROUP[i], :])
            if place == 0 and j + 3 < CHUNKS:
                flip_x(j + 3, 1 - i)
            if i == 0 and place == 0 and j + 2 < CHUNKS:
                pair_up(j + 2, nc.vector)
            if place == 1 and j + 1 < CHUNKS:
                quantise(i, j + 1, x_t[j + 1] if i == 0 else pair_t[j + 1])
            if step + PRODUCT_BANKS < len(passes):
                multiply(*passes[step + PRODUCT_BANKS])
            if i == 1 and place == 1:
                twice = rows[:].rearrange("p (g two) d -> p g two d", two=2)
                relu(1, twice[:, :, 0, :], twice[:, :, 0, :])
                pool_copy(twice[:, :, 1, :], twice[:, :, 0, :])
                store(1, j * CHUNK, rows[:])
            if i == 0 and place % 2 == 1:
                relu(0, rows[:, place - 1 : place + 1, :], rows[:, place - 1 : place + 1, :])
            if i == 0 and place == CHUNK - 1:
                store(0, j * CHUNK, rows[:])
